import numpy as np
import ml_dtypes


def mxq(x, axis, fmt="e4m3"):
    dtype, down = {"e4m3": (ml_dtypes.float8_e4m3fn, 7), "e5m2": (ml_dtypes.float8_e5m2, 14)}[fmt]
    v = np.moveaxis(np.asarray(x, np.float32).astype(ml_dtypes.bfloat16).astype(np.float64), axis, -1)
    blocks = v.reshape(v.shape[:-1] + (-1, 32))
    amax = np.abs(blocks).max(-1, keepdims=True)
    byte = np.maximum(np.where(amax > 0, np.frexp(amax)[1] - 1 + 127, 0) - down, 1)
    scale = np.exp2(byte - 127.0)
    codes = (blocks / scale).astype(np.float32).astype(dtype).astype(np.float64)
    return np.moveaxis((codes * scale).reshape(v.shape), -1, axis)


WIDE = False


def mx_kscale(k):
    if not WIDE:
        return np.ones(k)
    levels = np.array([10, -10, 5, -5, 0])
    if k % 512:
        return np.exp2(np.random.permutation(np.resize(levels, k // 32))).repeat(32)
    a = np.empty((k // 512, 16))
    for p in range(k // 512):
        a[p, :8] = np.random.permutation(np.resize(levels, 8))
        for g in range(8):
            far = levels[np.abs(levels - a[p, g]) >= 10]
            a[p, g + 8] = far[np.random.randint(len(far))]
    return np.exp2(a.ravel()).repeat(32)


BF16 = ml_dtypes.bfloat16


def bf(x):
    return np.asarray(x, np.float32).astype(BF16)


def f64(x):
    return np.asarray(x).astype(np.float64)


N1, N2, N3, R1, R = 16, 16, 512, 512, 8192


def setup_inputs():
    s = mx_kscale(R)
    g = R ** (-1.0 / 6.0)
    return {"X": bf(np.random.standard_normal((N1, N2, N3))),
            "A": bf(np.random.standard_normal((N1, R)) * g * s),
            "B": bf(np.random.standard_normal((N2, R)) * g),
            "C": bf(np.random.standard_normal((N3, R)) * g / s)}


def reference(X, A, B, C):
    p = (f64(A)[:, None, :] * f64(B)[None, :, :]).reshape(N1 * N2, R)
    approx = mxq(p, 1, "e4m3") @ mxq(f64(C), 1, "e4m3").T
    return approx.reshape(N1, N2, N3) - f64(X)

@@ -1,0 +1,181 @@
+from contextlib import ExitStack
+
+import concourse.mybir as mybir
+from concourse.masks import make_identity
+
+F32 = mybir.dt.float32
+BF16 = mybir.dt.bfloat16
+U32 = mybir.dt.uint32
+U8 = mybir.dt.uint8
+FP8X4 = mybir.dt.float8_e4m3fn_x4
+
+P = 128
+N1, N2, N3, R = 16, 16, 512, 8192
+PACK = 4
+K_PASS = P * PACK
+PASS_WORDS = K_PASS // 2
+PASSES = R // K_PASS
+ROUND_PASSES = 2
+ROUNDS = PASSES // ROUND_PASSES
+ROUND_R = ROUND_PASSES * K_PASS
+MX_BEHIND = 3
+FIRST_ROUNDS = 2
+OUT_COLS = 256
+M_TILES = N1 * N2 // P
+M_COLS = N1 * N2
+C_TILES = N3 // P
+SPLIT = P // N1
+
+FLOPS = 2 * N1 * N2 * N3 * R
+
+
+def tile_recon_loss_pa_kernel(tc, X, A, B, C, out):
+    nc = tc.nc
+    with ExitStack() as ctx:
+        keep = ctx.enter_context(tc.tile_pool(name="keep", bufs=1))
+        prod_pool = ctx.enter_context(tc.tile_pool(name="prod", bufs=3))
+        group_pool = ctx.enter_context(tc.tile_pool(name="group", bufs=6))
+        res_pool = ctx.enter_context(tc.tile_pool(name="res", bufs=4))
+        acc_pool = ctx.enter_context(tc.psum_pool(name="acc", bufs=1))
+        turn_pool = ctx.enter_context(tc.psum_pool(name="turn", bufs=6))
+
+        ctx.enter_context(tc.manual_schedule())
+
+        ident = keep.tile([P, P], F32)
+        make_identity(nc, ident[:])
+
+        a_raw = keep.tile([P, R // SPLIT], BF16)
+        nc.sync.dma_start(out=a_raw[:], in_=A.rearrange("i (x w) -> (i x) w", x=SPLIT))
+        b_raw = keep.tile([P, R // SPLIT], BF16)
+        nc.sync.dma_start(out=b_raw[:], in_=B.rearrange("j (x w) -> (j x) w", x=SPLIT))
+        c_view = C.rearrange("(a p) r -> p a r", p=P)
+        c_raw = []
+        for k in range(ROUNDS):
+            c_chunk = keep.tile([P, C_TILES, ROUND_R], BF16, name="c_raw%d" % k)
+            nc.sync.dma_start(out=c_chunk[:], in_=c_view[:, :, k * ROUND_R : (k + 1) * ROUND_R])
+            c_raw.append(c_chunk)
+        x_sb = keep.tile([P, M_TILES, N3], BF16)
+        nc.sync.dma_start(out=x_sb[:], in_=X.rearrange("(h i) j k -> (i j) h k", h=M_TILES))
+
+        def turn_factor(raw, turned, copy):
+            bank = turn_pool.tile([P, 4, P], F32, tag="bank", name="factor_bank")
+            words = raw[:].bitcast(F32)
+            for y in range(4):
+                yh, u = divmod(y, 2)
+                nc.tensor.transpose(
+                    bank[:, y, :], words[:, yh * PASS_WORDS + u : (yh + 1) * PASS_WORDS : 2], ident[:]
+                )
+            src = bank[:].rearrange("p (yh u) (i x) -> p yh x i u", u=2, x=SPLIT)
+            dst = turned[:].bitcast(F32).rearrange("p (x yh i u) -> p yh x i u", x=SPLIT, yh=2, u=2)
+            for pieces in (slice(0, FIRST_ROUNDS), slice(FIRST_ROUNDS, SPLIT)):
+                for yh in range(2):
+                    copy(out=dst[:, yh, pieces], in_=src[:, yh, pieces])
+
+        a_t = keep.tile([P, PASSES * N1 * PACK], BF16)
+        b_t = keep.tile([P, PASSES * N2 * PACK], BF16)
+        turn_factor(a_raw, a_t, nc.vector.tensor_copy)
+        turn_factor(b_raw, b_t, nc.scalar.copy)
+        a_by_pass = a_t[:].rearrange("p (g i t) -> p g i t", g=PASSES, i=N1)
+        b_by_pass = b_t[:].rearrange("p (g j t) -> p g j t", g=PASSES, j=N2)
+
+        p_prod = {}
+        p_codes = {}
+        p_scales = {}
+
+        def product(k):
+            passes = slice(k * ROUND_PASSES, (k + 1) * ROUND_PASSES)
+            full = [P, ROUND_PASSES, N1, N2, PACK]
+            prod = prod_pool.tile([P, ROUND_PASSES * M_COLS * PACK], BF16, align_bytes=64, name="prod")
+            nc.vector.tensor_tensor(
+                out=prod[:].rearrange("p (g i j t) -> p g i j t", g=ROUND_PASSES, i=N1, j=N2),
+                in0=a_by_pass[:, passes].unsqueeze(3).to_broadcast(full),
+                in1=b_by_pass[:, passes].unsqueeze(2).to_broadcast(full),
+                op=mybir.AluOpType.mult,
+            )
+            p_prod[k] = prod
+
+        def quantise_p(k):
+            codes = keep.tile([P, ROUND_PASSES * M_COLS], U32, align_bytes=64, name="p_codes%d" % k)
+            scales = keep.tile([P, ROUND_PASSES * M_COLS], U8, align_bytes=64, name="p_scales%d" % k)
+            nc.vector.quantize_mx(out=codes[:].bitcast(FP8X4), scales=scales[:], in_=p_prod[k][:])
+            p_codes[k] = codes
+            p_scales[k] = scales
+
+        c_grouped = {}
+        c_codes = {}
+        c_scales = {}
+
+        def turn_c(k):
+            for g_local in range(ROUND_PASSES):
+                grouped = group_pool.tile([P, N3 * PACK], BF16, align_bytes=64, name="grouped")
+                grouped_words = grouped[:].bitcast(F32)
+                for half in range(2):
+                    bank = turn_pool.tile([P, 2, 2 * P], F32, tag="bank", name="c_bank")
+                    for a in range(2):
+                        words = c_raw[k][:, 2 * half + a, :].bitcast(F32)
+                        for u in range(2):
+                            first = g_local * PASS_WORDS
+                            nc.tensor.transpose(
+                                bank[:, u, a * P : (a + 1) * P],
+                                words[:, first + u : first + PASS_WORDS : 2],
+                                ident[:],
+                            )
+                    nc.scalar.copy(
+                        out=grouped_words[:, half * 4 * P : (half + 1) * 4 * P].rearrange(
+                            "p (n u) -> p n u", u=2
+                        ),
+                        in_=bank[:].rearrange("p u n -> p n u"),
+                    )
+                c_grouped[k * ROUND_PASSES + g_local] = grouped
+
+        def quantise_c(g):
+            codes = keep.tile([P, N3], U32, align_bytes=64, name="c_codes%d" % g)
+            scales = keep.tile([P, N3], U8, align_bytes=64, name="c_scales%d" % g)
+            nc.vector.quantize_mx(out=codes[:].bitcast(FP8X4), scales=scales[:], in_=c_grouped[g][:])
+            c_codes[g] = codes
+            c_scales[g] = scales
+
+        acc = [acc_pool.tile([P, N3], F32, name="acc%d" % h) for h in range(M_TILES)]
+
+        def multiply(g):
+            k, g_local = divmod(g, ROUND_PASSES)
+            for h in range(M_TILES):
+                cols = slice(g_local * M_COLS + h * P, g_local * M_COLS + (h + 1) * P)
+                nc.tensor.matmul_mx(
+                    out=acc[h][:],
+                    lhsT=p_codes[k][:, cols].bitcast(FP8X4),
+                    lhsT_scale=p_scales[k][:, cols],
+                    rhs=c_codes[g][:].bitcast(FP8X4),
+                    rhs_scale=c_scales[g][:],
+                    start=(g == 0),
+                    stop=(g == PASSES - 1),
+                )
+
+        for k in range(FIRST_ROUNDS):
+            product(k)
+        quantise_p(0)
+        for s in range(ROUNDS + 2):
+            if s < ROUNDS:
+                turn_c(s)
+            m = s - 1
+            if 0 <= m < ROUNDS:
+                if m + FIRST_ROUNDS < ROUNDS:
+                    product(m + FIRST_ROUNDS)
+                quantise_c(ROUND_PASSES * m)
+                if m + 1 < ROUNDS:
+                    quantise_p(m + 1)
+                quantise_c(ROUND_PASSES * m + 1)
+            last_turned = ROUND_PASSES * (s + 1) - 1
+            for g in range(last_turned - MX_BEHIND - 1, last_turned - MX_BEHIND + 1):
+                if 0 <= g < PASSES:
+                    multiply(g)
+
+        out_view = out.rearrange("(h i) j k -> h (i j) k", h=M_TILES)
+        for h in range(M_TILES):
+            for first in range(0, N3, OUT_COLS):
+                cols = slice(first, first + OUT_COLS)
+                res = res_pool.tile([P, OUT_COLS], F32, name="res")
+                nc.vector.tensor_tensor(
+                    out=res[:], in0=acc[h][:, cols], in1=x_sb[:, h, cols], op=mybir.AluOpType.subtract
+                )
+                nc.sync.dma_start(out=out_view[h][:, cols], in_=res[:])

@@ -20,6 +20,7 @@ ROUNDS = PASSES // ROUND_PASSES
 ROUND_R = ROUND_PASSES * K_PASS
 MX_BEHIND = 3
 FIRST_ROUNDS = 2
+FINE_ROUNDS = 2
 OUT_COLS = 256
 M_TILES = N1 * N2 // P
 M_COLS = N1 * N2
@@ -34,7 +35,7 @@ def tile_recon_loss_pa_kernel(tc, X, A, B, C, out):
     with ExitStack() as ctx:
         keep = ctx.enter_context(tc.tile_pool(name="keep", bufs=1))
         prod_pool = ctx.enter_context(tc.tile_pool(name="prod", bufs=3))
-        group_pool = ctx.enter_context(tc.tile_pool(name="group", bufs=6))
+        group_pool = ctx.enter_context(tc.tile_pool(name="group", bufs=3))
         res_pool = ctx.enter_context(tc.tile_pool(name="res", bufs=4))
         acc_pool = ctx.enter_context(tc.psum_pool(name="acc", bufs=1))
         turn_pool = ctx.enter_context(tc.psum_pool(name="turn", bufs=6))
@@ -51,9 +52,18 @@ def tile_recon_loss_pa_kernel(tc, X, A, B, C, out):
         c_view = C.rearrange("(a p) r -> p a r", p=P)
         c_raw = []
         for k in range(ROUNDS):
-            c_chunk = keep.tile([P, C_TILES, ROUND_R], BF16, name="c_raw%d" % k)
-            nc.sync.dma_start(out=c_chunk[:], in_=c_view[:, :, k * ROUND_R : (k + 1) * ROUND_R])
-            c_raw.append(c_chunk)
+            r_cols = slice(k * ROUND_R, (k + 1) * ROUND_R)
+            if k < FINE_ROUNDS:
+                pieces = []
+                for a in range(C_TILES):
+                    c_piece = keep.tile([P, ROUND_R], BF16, name="c_raw%d_%d" % (k, a))
+                    nc.sync.dma_start(out=c_piece[:], in_=c_view[:, a, r_cols])
+                    pieces.append(c_piece[:])
+            else:
+                c_chunk = keep.tile([P, C_TILES, ROUND_R], BF16, name="c_raw%d" % k)
+                nc.sync.dma_start(out=c_chunk[:], in_=c_view[:, :, r_cols])
+                pieces = [c_chunk[:, a, :] for a in range(C_TILES)]
+            c_raw.append(pieces)
         x_sb = keep.tile([P, M_TILES, N3], BF16)
         nc.sync.dma_start(out=x_sb[:], in_=X.rearrange("(h i) j k -> (i j) h k", h=M_TILES))
 
@@ -106,32 +116,29 @@ def tile_recon_loss_pa_kernel(tc, X, A, B, C, out):
         c_scales = {}
 
         def turn_c(k):
-            for g_local in range(ROUND_PASSES):
-                grouped = group_pool.tile([P, N3 * PACK], BF16, align_bytes=64, name="grouped")
-                grouped_words = grouped[:].bitcast(F32)
-                for half in range(2):
-                    bank = turn_pool.tile([P, 2, 2 * P], F32, tag="bank", name="c_bank")
-                    for a in range(2):
-                        words = c_raw[k][:, 2 * half + a, :].bitcast(F32)
-                        for u in range(2):
-                            first = g_local * PASS_WORDS
-                            nc.tensor.transpose(
-                                bank[:, u, a * P : (a + 1) * P],
-                                words[:, first + u : first + PASS_WORDS : 2],
-                                ident[:],
-                            )
-                    nc.scalar.copy(
-                        out=grouped_words[:, half * 4 * P : (half + 1) * 4 * P].rearrange(
-                            "p (n u) -> p n u", u=2
-                        ),
-                        in_=bank[:].rearrange("p u n -> p n u"),
-                    )
-                c_grouped[k * ROUND_PASSES + g_local] = grouped
+            grouped = group_pool.tile([P, ROUND_PASSES * N3 * PACK], BF16, align_bytes=64, name="grouped")
+            grouped_words = grouped[:].bitcast(F32).rearrange("p (g n u) -> p g n u", g=ROUND_PASSES, u=2)
+            for a in range(C_TILES):
+                bank = turn_pool.tile([P, ROUND_PASSES, 2, P], F32, tag="bank", name="c_bank")
+                words = c_raw[k][a].bitcast(F32)
+                for g_local in range(ROUND_PASSES):
+                    first = g_local * PASS_WORDS
+                    for u in range(2):
+                        nc.tensor.transpose(
+                            bank[:, g_local, u, :], words[:, first + u : first + PASS_WORDS : 2], ident[:]
+                        )
+                nc.scalar.copy(
+                    out=grouped_words[:, :, a * P : (a + 1) * P, :],
+                    in_=bank[:].rearrange("p g u n -> p g n u"),
+                )
+            c_grouped[k] = grouped
 
         def quantise_c(g):
             codes = keep.tile([P, N3], U32, align_bytes=64, name="c_codes%d" % g)
             scales = keep.tile([P, N3], U8, align_bytes=64, name="c_scales%d" % g)
-            nc.vector.quantize_mx(out=codes[:].bitcast(FP8X4), scales=scales[:], in_=c_grouped[g][:])
+            k, g_local = divmod(g, ROUND_PASSES)
+            cols = slice(g_local * N3 * PACK, (g_local + 1) * N3 * PACK)
+            nc.vector.quantize_mx(out=codes[:].bitcast(FP8X4), scales=scales[:], in_=c_grouped[k][:, cols])
             c_codes[g] = codes
             c_scales[g] = scales
 

@@ -20,7 +20,7 @@ ROUNDS = PASSES // ROUND_PASSES
 ROUND_R = ROUND_PASSES * K_PASS
 MX_BEHIND = 3
 FIRST_ROUNDS = 2
-FINE_ROUNDS = 2
+FINE_ROUNDS = 4
 OUT_COLS = 256
 M_TILES = N1 * N2 // P
 M_COLS = N1 * N2

@@ -19,7 +19,9 @@ ROUND_PASSES = 2
 ROUNDS = PASSES // ROUND_PASSES
 ROUND_R = ROUND_PASSES * K_PASS
 MX_BEHIND = 3
-FIRST_ROUNDS = 2
+PAIR = 2
+FIRST_ROUNDS = PAIR
+FIRST_PRODUCTS = 3
 FINE_ROUNDS = 4
 OUT_COLS = 256
 M_TILES = N1 * N2 // P
@@ -45,10 +47,13 @@ def tile_recon_loss_pa_kernel(tc, X, A, B, C, out):
         ident = keep.tile([P, P], F32)
         make_identity(nc, ident[:])
 
-        a_raw = keep.tile([P, R // SPLIT], BF16)
-        nc.sync.dma_start(out=a_raw[:], in_=A.rearrange("i (x w) -> (i x) w", x=SPLIT))
-        b_raw = keep.tile([P, R // SPLIT], BF16)
-        nc.sync.dma_start(out=b_raw[:], in_=B.rearrange("j (x w) -> (j x) w", x=SPLIT))
+        factor_views = [factor.rearrange("i (x w) -> (i x) w", x=SPLIT) for factor in (A, B)]
+        factor_raw = {}
+        for yh in range(ROUND_PASSES):
+            for f in range(2):
+                raw = keep.tile([P, K_PASS], BF16, name="factor_raw%d_%d" % (f, yh))
+                nc.sync.dma_start(out=raw[:], in_=factor_views[f][:, yh * K_PASS : (yh + 1) * K_PASS])
+                factor_raw[(f, yh)] = raw
         c_view = C.rearrange("(a p) r -> p a r", p=P)
         c_raw = []
         for k in range(ROUNDS):
@@ -67,47 +72,52 @@ def tile_recon_loss_pa_kernel(tc, X, A, B, C, out):
         x_sb = keep.tile([P, M_TILES, N3], BF16)
         nc.sync.dma_start(out=x_sb[:], in_=X.rearrange("(h i) j k -> (i j) h k", h=M_TILES))
 
-        def turn_factor(raw, turned, copy):
-            bank = turn_pool.tile([P, 4, P], F32, tag="bank", name="factor_bank")
-            words = raw[:].bitcast(F32)
-            for y in range(4):
-                yh, u = divmod(y, 2)
-                nc.tensor.transpose(
-                    bank[:, y, :], words[:, yh * PASS_WORDS + u : (yh + 1) * PASS_WORDS : 2], ident[:]
-                )
-            src = bank[:].rearrange("p (yh u) (i x) -> p yh x i u", u=2, x=SPLIT)
-            dst = turned[:].bitcast(F32).rearrange("p (x yh i u) -> p yh x i u", x=SPLIT, yh=2, u=2)
-            for pieces in (slice(0, FIRST_ROUNDS), slice(FIRST_ROUNDS, SPLIT)):
-                for yh in range(2):
-                    copy(out=dst[:, yh, pieces], in_=src[:, yh, pieces])
-
         a_t = keep.tile([P, PASSES * N1 * PACK], BF16)
         b_t = keep.tile([P, PASSES * N2 * PACK], BF16)
-        turn_factor(a_raw, a_t, nc.vector.tensor_copy)
-        turn_factor(b_raw, b_t, nc.scalar.copy)
-        a_by_pass = a_t[:].rearrange("p (g i t) -> p g i t", g=PASSES, i=N1)
-        b_by_pass = b_t[:].rearrange("p (g j t) -> p g j t", g=PASSES, j=N2)
+        for yh in range(ROUND_PASSES):
+            sides = []
+            for f, turned in enumerate((a_t, b_t)):
+                bank = turn_pool.tile([P, 2, P], F32, tag="bank", name="factor_bank")
+                words = factor_raw[(f, yh)][:].bitcast(F32)
+                for u in range(2):
+                    nc.tensor.transpose(bank[:, u, :], words[:, u : PASS_WORDS : 2], ident[:])
+                src = bank[:].rearrange("p u (i x) -> p x i u", x=SPLIT)
+                dst = turned[:].bitcast(F32).rearrange("p (yh x i u) -> p yh x i u", x=SPLIT, yh=2, u=2)
+                sides.append((src, dst[:, yh]))
+            for pieces in (slice(0, FIRST_ROUNDS), slice(FIRST_ROUNDS, SPLIT)):
+                for src, dst in sides:
+                    nc.scalar.copy(out=dst[:, pieces], in_=src[:, pieces])
+        a_by_half = a_t[:].rearrange("p (yh x i t) -> p yh x i t", yh=ROUND_PASSES, i=N1, t=PACK)
+        b_by_half = b_t[:].rearrange("p (yh x j t) -> p yh x j t", yh=ROUND_PASSES, j=N2, t=PACK)
 
-        p_prod = {}
+        p_pair = {}
         p_codes = {}
         p_scales = {}
 
-        def product(k):
-            passes = slice(k * ROUND_PASSES, (k + 1) * ROUND_PASSES)
-            full = [P, ROUND_PASSES, N1, N2, PACK]
-            prod = prod_pool.tile([P, ROUND_PASSES * M_COLS * PACK], BF16, align_bytes=64, name="prod")
+        def product(n):
+            q, yh = divmod(n, ROUND_PASSES)
+            if yh == 0:
+                p_pair[q] = prod_pool.tile([P, PAIR * ROUND_PASSES * M_COLS * PACK], BF16, align_bytes=64, name="prod")
+            rounds = slice(q * PAIR, (q + 1) * PAIR)
+            full = [P, PAIR, N1, N2, PACK]
+            by_half = p_pair[q][:].rearrange("p (k yh i j t) -> p yh k i j t", k=PAIR, yh=ROUND_PASSES, i=N1, j=N2)
             nc.vector.tensor_tensor(
-                out=prod[:].rearrange("p (g i j t) -> p g i j t", g=ROUND_PASSES, i=N1, j=N2),
-                in0=a_by_pass[:, passes].unsqueeze(3).to_broadcast(full),
-                in1=b_by_pass[:, passes].unsqueeze(2).to_broadcast(full),
+                out=by_half[:, yh],
+                in0=a_by_half[:, yh, rounds].unsqueeze(3).to_broadcast(full),
+                in1=b_by_half[:, yh, rounds].unsqueeze(2).to_broadcast(full),
                 op=mybir.AluOpType.mult,
             )
-            p_prod[k] = prod
 
         def quantise_p(k):
             codes = keep.tile([P, ROUND_PASSES * M_COLS], U32, align_bytes=64, name="p_codes%d" % k)
             scales = keep.tile([P, ROUND_PASSES * M_COLS], U8, align_bytes=64, name="p_scales%d" % k)
-            nc.vector.quantize_mx(out=codes[:].bitcast(FP8X4), scales=scales[:], in_=p_prod[k][:])
+            q, k_local = divmod(k, PAIR)
+            width = ROUND_PASSES * M_COLS * PACK
+            nc.vector.quantize_mx(
+                out=codes[:].bitcast(FP8X4),
+                scales=scales[:],
+                in_=p_pair[q][:, k_local * width : (k_local + 1) * width],
+            )
             p_codes[k] = codes
             p_scales[k] = scales
 
@@ -158,16 +168,16 @@ def tile_recon_loss_pa_kernel(tc, X, A, B, C, out):
                     stop=(g == PASSES - 1),
                 )
 
-        for k in range(FIRST_ROUNDS):
-            product(k)
+        for n in range(FIRST_PRODUCTS):
+            product(n)
         quantise_p(0)
         for s in range(ROUNDS + 2):
             if s < ROUNDS:
                 turn_c(s)
             m = s - 1
             if 0 <= m < ROUNDS:
-                if m + FIRST_ROUNDS < ROUNDS:
-                    product(m + FIRST_ROUNDS)
+                if 0 < m and m + FIRST_PRODUCTS - 1 < ROUNDS:
+                    product(m + FIRST_PRODUCTS - 1)
                 quantise_c(ROUND_PASSES * m)
                 if m + 1 < ROUNDS:
                     quantise_p(m + 1)

@@ -22,6 +22,7 @@ MX_BEHIND = 3
 PAIR = 2
 FIRST_ROUNDS = PAIR
 FIRST_PRODUCTS = 3
+SORTED_UNITS = ((2, 1), (3, 0), (3, 1))
 FINE_ROUNDS = 4
 OUT_COLS = 256
 M_TILES = N1 * N2 // P
@@ -39,6 +40,7 @@ def tile_recon_loss_pa_kernel(tc, X, A, B, C, out):
         prod_pool = ctx.enter_context(tc.tile_pool(name="prod", bufs=3))
         group_pool = ctx.enter_context(tc.tile_pool(name="group", bufs=3))
         res_pool = ctx.enter_context(tc.tile_pool(name="res", bufs=4))
+        sort_pool = ctx.enter_context(tc.tile_pool(name="sort", bufs=3))
         acc_pool = ctx.enter_context(tc.psum_pool(name="acc", bufs=1))
         turn_pool = ctx.enter_context(tc.psum_pool(name="turn", bufs=6))
 
@@ -125,6 +127,15 @@ def tile_recon_loss_pa_kernel(tc, X, A, B, C, out):
         c_codes = {}
         c_scales = {}
 
+        c_sorted = {}
+
+        def sort_c(k):
+            sorted_words = sort_pool.tile([P, len(SORTED_UNITS), 2, P], F32, name="sorted_words")
+            for unit, (a, g_local) in enumerate(SORTED_UNITS):
+                words = c_raw[k][a].bitcast(F32)[:, g_local * PASS_WORDS : (g_local + 1) * PASS_WORDS]
+                nc.scalar.copy(out=sorted_words[:, unit], in_=words.rearrange("p (w u) -> p u w", u=2))
+            c_sorted[k] = sorted_words
+
         def turn_c(k):
             grouped = group_pool.tile([P, ROUND_PASSES * N3 * PACK], BF16, align_bytes=64, name="grouped")
             grouped_words = grouped[:].bitcast(F32).rearrange("p (g n u) -> p g n u", g=ROUND_PASSES, u=2)
@@ -134,9 +145,11 @@ def tile_recon_loss_pa_kernel(tc, X, A, B, C, out):
                 for g_local in range(ROUND_PASSES):
                     first = g_local * PASS_WORDS
                     for u in range(2):
-                        nc.tensor.transpose(
-                            bank[:, g_local, u, :], words[:, first + u : first + PASS_WORDS : 2], ident[:]
-                        )
+                        if k in c_sorted and (a, g_local) in SORTED_UNITS:
+                            turned_words = c_sorted[k][:, SORTED_UNITS.index((a, g_local)), u, :]
+                        else:
+                            turned_words = words[:, first + u : first + PASS_WORDS : 2]
+                        nc.tensor.transpose(bank[:, g_local, u, :], turned_words, ident[:])
                 nc.scalar.copy(
                     out=grouped_words[:, :, a * P : (a + 1) * P, :],
                     in_=bank[:].rearrange("p g u n -> p g n u"),
@@ -174,6 +187,8 @@ def tile_recon_loss_pa_kernel(tc, X, A, B, C, out):
         for s in range(ROUNDS + 2):
             if s < ROUNDS:
                 turn_c(s)
+            if s + 1 < ROUNDS:
+                sort_c(s + 1)
             m = s - 1
             if 0 <= m < ROUNDS:
                 if 0 < m and m + FIRST_PRODUCTS - 1 < ROUNDS:

@@ -22,7 +22,12 @@ MX_BEHIND = 3
 PAIR = 2
 FIRST_ROUNDS = PAIR
 FIRST_PRODUCTS = 3
-SORTED_UNITS = ((2, 1), (3, 0), (3, 1))
+SCALAR_SORTS = ((3, 0), (3, 1))
+SCALAR_SORTS_FROM = 3
+VECTOR_SORTS = ((2, 1),)
+VECTOR_SORTS_FROM = 3
+TAIL_PASSES = 2
+LAST_HALVES = 2
 FINE_ROUNDS = 4
 OUT_COLS = 256
 M_TILES = N1 * N2 // P
@@ -41,6 +46,7 @@ def tile_recon_loss_pa_kernel(tc, X, A, B, C, out):
         group_pool = ctx.enter_context(tc.tile_pool(name="group", bufs=3))
         res_pool = ctx.enter_context(tc.tile_pool(name="res", bufs=4))
         sort_pool = ctx.enter_context(tc.tile_pool(name="sort", bufs=3))
+        last_pool = ctx.enter_context(tc.tile_pool(name="last", bufs=1))
         acc_pool = ctx.enter_context(tc.psum_pool(name="acc", bufs=1))
         turn_pool = ctx.enter_context(tc.psum_pool(name="turn", bufs=6))
 
@@ -129,47 +135,64 @@ def tile_recon_loss_pa_kernel(tc, X, A, B, C, out):
 
         c_sorted = {}
 
-        def sort_c(k):
-            sorted_words = sort_pool.tile([P, len(SORTED_UNITS), 2, P], F32, name="sorted_words")
-            for unit, (a, g_local) in enumerate(SORTED_UNITS):
-                words = c_raw[k][a].bitcast(F32)[:, g_local * PASS_WORDS : (g_local + 1) * PASS_WORDS]
-                nc.scalar.copy(out=sorted_words[:, unit], in_=words.rearrange("p (w u) -> p u w", u=2))
-            c_sorted[k] = sorted_words
+        def sort_c(k, units, copy):
+            a = units[0][0]
+            first = units[0][1] * PASS_WORDS
+            sorted_words = sort_pool.tile([P, len(units), 2, P], F32, name="sorted%d" % len(units))
+            words = c_raw[k][a].bitcast(F32)[:, first : first + len(units) * PASS_WORDS]
+            copy(out=sorted_words[:], in_=words.rearrange("p (g w u) -> p g u w", g=len(units), u=2))
+            for unit, (a, g_local) in enumerate(units):
+                c_sorted[(k, a, g_local)] = sorted_words[:, unit]
 
         def turn_c(k):
-            grouped = group_pool.tile([P, ROUND_PASSES * N3 * PACK], BF16, align_bytes=64, name="grouped")
-            grouped_words = grouped[:].bitcast(F32).rearrange("p (g n u) -> p g n u", g=ROUND_PASSES, u=2)
-            for a in range(C_TILES):
-                bank = turn_pool.tile([P, ROUND_PASSES, 2, P], F32, tag="bank", name="c_bank")
-                words = c_raw[k][a].bitcast(F32)
-                for g_local in range(ROUND_PASSES):
-                    first = g_local * PASS_WORDS
-                    for u in range(2):
-                        if k in c_sorted and (a, g_local) in SORTED_UNITS:
-                            turned_words = c_sorted[k][:, SORTED_UNITS.index((a, g_local)), u, :]
-                        else:
-                            turned_words = words[:, first + u : first + PASS_WORDS : 2]
-                        nc.tensor.transpose(bank[:, g_local, u, :], turned_words, ident[:])
-                nc.scalar.copy(
-                    out=grouped_words[:, :, a * P : (a + 1) * P, :],
-                    in_=bank[:].rearrange("p g u n -> p g n u"),
-                )
-            c_grouped[k] = grouped
+            halves = LAST_HALVES if k == ROUNDS - 1 else 1
+            half_tiles = C_TILES // halves
+            c_grouped[k] = []
+            for half in range(halves):
+                if halves == 1:
+                    grouped = group_pool.tile([P, ROUND_PASSES * N3 * PACK], BF16, align_bytes=64, name="grouped")
+                else:
+                    grouped = last_pool.tile(
+                        [P, ROUND_PASSES * N3 * PACK // halves], BF16, align_bytes=64, name="last_grouped%d" % half
+                    )
+                c_grouped[k].append(grouped)
+                grouped_words = grouped[:].bitcast(F32).rearrange("p (g n u) -> p g n u", g=ROUND_PASSES, u=2)
+                for a_local in range(half_tiles):
+                    a = half * half_tiles + a_local
+                    bank = turn_pool.tile([P, ROUND_PASSES, 2, P], F32, tag="bank", name="c_bank")
+                    words = c_raw[k][a].bitcast(F32)
+                    for g_local in range(ROUND_PASSES):
+                        first = g_local * PASS_WORDS
+                        for u in range(2):
+                            if (k, a, g_local) in c_sorted:
+                                turned_words = c_sorted[(k, a, g_local)][:, u, :]
+                            else:
+                                turned_words = words[:, first + u : first + PASS_WORDS : 2]
+                            nc.tensor.transpose(bank[:, g_local, u, :], turned_words, ident[:])
+                    nc.scalar.copy(
+                        out=grouped_words[:, :, a_local * P : (a_local + 1) * P, :],
+                        in_=bank[:].rearrange("p g u n -> p g n u"),
+                    )
 
-        def quantise_c(g):
-            codes = keep.tile([P, N3], U32, align_bytes=64, name="c_codes%d" % g)
-            scales = keep.tile([P, N3], U8, align_bytes=64, name="c_scales%d" % g)
+        def new_c_codes(g):
+            c_codes[g] = keep.tile([P, N3], U32, align_bytes=64, name="c_codes%d" % g)
+            c_scales[g] = keep.tile([P, N3], U8, align_bytes=64, name="c_scales%d" % g)
+
+        def quantise_c(g, half):
             k, g_local = divmod(g, ROUND_PASSES)
-            cols = slice(g_local * N3 * PACK, (g_local + 1) * N3 * PACK)
-            nc.vector.quantize_mx(out=codes[:].bitcast(FP8X4), scales=scales[:], in_=c_grouped[k][:, cols])
-            c_codes[g] = codes
-            c_scales[g] = scales
+            rows = N3 // len(c_grouped[k])
+            cols = slice(half * rows, (half + 1) * rows)
+            nc.vector.quantize_mx(
+                out=c_codes[g][:, cols].bitcast(FP8X4),
+                scales=c_scales[g][:, cols],
+                in_=c_grouped[k][half][:, g_local * rows * PACK : (g_local + 1) * rows * PACK],
+            )
 
         acc = [acc_pool.tile([P, N3], F32, name="acc%d" % h) for h in range(M_TILES)]
 
-        def multiply(g):
+        def multiply(g, m_tiles):
             k, g_local = divmod(g, ROUND_PASSES)
-            for h in range(M_TILES):
+            for h in m_tiles:
                 cols = slice(g_local * M_COLS + h * P, g_local * M_COLS + (h + 1) * P)
                 nc.tensor.matmul_mx(
                     out=acc[h][:],
@@ -187,20 +210,31 @@ def tile_recon_loss_pa_kernel(tc, X, A, B, C, out):
         for s in range(ROUNDS + 2):
             if s < ROUNDS:
                 turn_c(s)
-            if s + 1 < ROUNDS:
-                sort_c(s + 1)
+            if SCALAR_SORTS_FROM <= s + 1 < ROUNDS:
+                sort_c(s + 1, SCALAR_SORTS, nc.scalar.copy)
             m = s - 1
             if 0 <= m < ROUNDS:
+                for g_local in range(ROUND_PASSES):
+                    new_c_codes(ROUND_PASSES * m + g_local)
                 if 0 < m and m + FIRST_PRODUCTS - 1 < ROUNDS:
                     product(m + FIRST_PRODUCTS - 1)
-                quantise_c(ROUND_PASSES * m)
-                if m + 1 < ROUNDS:
+                if m < ROUNDS - 1:
+                    quantise_c(ROUND_PASSES * m, 0)
                     quantise_p(m + 1)
-                quantise_c(ROUND_PASSES * m + 1)
+                    quantise_c(ROUND_PASSES * m + 1, 0)
+                else:
+                    for half in range(LAST_HALVES):
+                        for g_local in range(ROUND_PASSES):
+                            quantise_c(ROUND_PASSES * m + g_local, half)
+                if VECTOR_SORTS_FROM <= m + 2 < ROUNDS:
+                    sort_c(m + 2, VECTOR_SORTS, nc.vector.tensor_copy)
             last_turned = ROUND_PASSES * (s + 1) - 1
             for g in range(last_turned - MX_BEHIND - 1, last_turned - MX_BEHIND + 1):
-                if 0 <= g < PASSES:
-                    multiply(g)
+                if 0 <= g < PASSES - TAIL_PASSES:
+                    multiply(g, range(M_TILES))
+        for h in range(M_TILES):
+            for g in range(PASSES - TAIL_PASSES, PASSES):
+                multiply(g, [h])
 
         out_view = out.rearrange("(h i) j k -> h (i j) k", h=M_TILES)
         for h in range(M_TILES):

@@ -23,9 +23,8 @@ PAIR = 2
 FIRST_ROUNDS = PAIR
 FIRST_PRODUCTS = 3
 SCALAR_SORTS = ((3, 0), (3, 1))
-SCALAR_SORTS_FROM = 3
-VECTOR_SORTS = ((2, 1),)
-VECTOR_SORTS_FROM = 3
+SHARED_SORTS = ((2, 1),)
+SORTS_FROM = 3
 TAIL_PASSES = 2
 LAST_HALVES = 2
 FINE_ROUNDS = 4
@@ -210,7 +209,9 @@ def tile_recon_loss_pa_kernel(tc, X, A, B, C, out):
         for s in range(ROUNDS + 2):
             if s < ROUNDS:
                 turn_c(s)
-            if SCALAR_SORTS_FROM <= s + 1 < ROUNDS:
+            if SORTS_FROM <= s + 1 < ROUNDS:
+                if (s + 1) % 2 == 1:
+                    sort_c(s + 1, SHARED_SORTS, nc.scalar.copy)
                 sort_c(s + 1, SCALAR_SORTS, nc.scalar.copy)
             m = s - 1
             if 0 <= m < ROUNDS:
@@ -226,8 +227,8 @@ def tile_recon_loss_pa_kernel(tc, X, A, B, C, out):
                     for half in range(LAST_HALVES):
                         for g_local in range(ROUND_PASSES):
                             quantise_c(ROUND_PASSES * m + g_local, half)
-                if VECTOR_SORTS_FROM <= m + 2 < ROUNDS:
-                    sort_c(m + 2, VECTOR_SORTS, nc.vector.tensor_copy)
+                if SORTS_FROM <= m + 2 < ROUNDS and (m + 2) % 2 == 0:
+                    sort_c(m + 2, SHARED_SORTS, nc.vector.tensor_copy)
             last_turned = ROUND_PASSES * (s + 1) - 1
             for g in range(last_turned - MX_BEHIND - 1, last_turned - MX_BEHIND + 1):
                 if 0 <= g < PASSES - TAIL_PASSES:

@@ -30,6 +30,7 @@ LAST_HALVES = 2
 FINE_ROUNDS = 4
 OUT_COLS = 256
 M_TILES = N1 * N2 // P
+SUMS = ((0, 0, 256), (1, 0, 256), (0, 256, 256), (1, 256, 256))
 M_COLS = N1 * N2
 C_TILES = N3 // P
 SPLIT = P // N1
@@ -47,7 +48,7 @@ def tile_recon_loss_pa_kernel(tc, X, A, B, C, out):
         sort_pool = ctx.enter_context(tc.tile_pool(name="sort", bufs=3))
         last_pool = ctx.enter_context(tc.tile_pool(name="last", bufs=1))
         acc_pool = ctx.enter_context(tc.psum_pool(name="acc", bufs=1))
-        turn_pool = ctx.enter_context(tc.psum_pool(name="turn", bufs=6))
+        turn_pool = ctx.enter_context(tc.psum_pool(name="turn", bufs=4))
 
         ctx.enter_context(tc.manual_schedule())
 
@@ -187,18 +188,22 @@ def tile_recon_loss_pa_kernel(tc, X, A, B, C, out):
                 in_=c_grouped[k][half][:, g_local * rows * PACK : (g_local + 1) * rows * PACK],
             )
 
-        acc = [acc_pool.tile([P, N3], F32, name="acc%d" % h) for h in range(M_TILES)]
+        acc = []
+        for number, (h, first, width) in enumerate(SUMS):
+            acc.append(acc_pool.tile([P, width], F32, name="acc%d" % number))
 
-        def multiply(g, m_tiles):
+        def multiply(g, sums):
             k, g_local = divmod(g, ROUND_PASSES)
-            for h in m_tiles:
+            for number in sums:
+                h, first, width = SUMS[number]
                 cols = slice(g_local * M_COLS + h * P, g_local * M_COLS + (h + 1) * P)
+                c_cols = slice(first, first + width)
                 nc.tensor.matmul_mx(
-                    out=acc[h][:],
+                    out=acc[number][:],
                     lhsT=p_codes[k][:, cols].bitcast(FP8X4),
                     lhsT_scale=p_scales[k][:, cols],
-                    rhs=c_codes[g][:].bitcast(FP8X4),
-                    rhs_scale=c_scales[g][:],
+                    rhs=c_codes[g][:, c_cols].bitcast(FP8X4),
+                    rhs_scale=c_scales[g][:, c_cols],
                     start=(g == 0),
                     stop=(g == PASSES - 1),
                 )
@@ -232,17 +237,20 @@ def tile_recon_loss_pa_kernel(tc, X, A, B, C, out):
             last_turned = ROUND_PASSES * (s + 1) - 1
             for g in range(last_turned - MX_BEHIND - 1, last_turned - MX_BEHIND + 1):
                 if 0 <= g < PASSES - TAIL_PASSES:
-                    multiply(g, range(M_TILES))
-        for h in range(M_TILES):
+                    multiply(g, range(len(SUMS)))
+        for number in range(len(SUMS)):
             for g in range(PASSES - TAIL_PASSES, PASSES):
-                multiply(g, [h])
+                multiply(g, [number])
 
         out_view = out.rearrange("(h i) j k -> h (i j) k", h=M_TILES)
-        for h in range(M_TILES):
-            for first in range(0, N3, OUT_COLS):
-                cols = slice(first, first + OUT_COLS)
+        for number, (h, start, width) in enumerate(SUMS):
+            for first in range(0, width, OUT_COLS):
+                cols = slice(start + first, start + first + OUT_COLS)
                 res = res_pool.tile([P, OUT_COLS], F32, name="res")
                 nc.vector.tensor_tensor(
-                    out=res[:], in0=acc[h][:, cols], in1=x_sb[:, h, cols], op=mybir.AluOpType.subtract
+                    out=res[:],
+                    in0=acc[number][:, first : first + OUT_COLS],
+                    in1=x_sb[:, h, cols],
+                    op=mybir.AluOpType.subtract,
                 )
                 nc.sync.dma_start(out=out_view[h][:, cols], in_=res[:])

@@ -27,10 +27,11 @@ SHARED_SORTS = ((2, 1),)
 SORTS_FROM = 3
 TAIL_PASSES = 2
 LAST_HALVES = 2
-FINE_ROUNDS = 4
+FINE_ROUNDS = 5
 OUT_COLS = 256
 M_TILES = N1 * N2 // P
 SUMS = ((0, 0, 256), (1, 0, 256), (0, 256, 256), (1, 256, 256))
+WEIGHT_ORDER = (0, 2, 1, 3)
 M_COLS = N1 * N2
 C_TILES = N3 // P
 SPLIT = P // N1
@@ -237,7 +238,7 @@ def tile_recon_loss_pa_kernel(tc, X, A, B, C, out):
             last_turned = ROUND_PASSES * (s + 1) - 1
             for g in range(last_turned - MX_BEHIND - 1, last_turned - MX_BEHIND + 1):
                 if 0 <= g < PASSES - TAIL_PASSES:
-                    multiply(g, range(len(SUMS)))
+                    multiply(g, WEIGHT_ORDER)
         for number in range(len(SUMS)):
             for g in range(PASSES - TAIL_PASSES, PASSES):
                 multiply(g, [number])

from contextlib import ExitStack

import concourse.mybir as mybir
from concourse.masks import make_identity

F32 = mybir.dt.float32
BF16 = mybir.dt.bfloat16
U32 = mybir.dt.uint32
U8 = mybir.dt.uint8
FP8X4 = mybir.dt.float8_e4m3fn_x4

P = 128
N1, N2, N3, R = 16, 16, 512, 8192
PACK = 4
K_PASS = P * PACK
PASS_WORDS = K_PASS // 2
PASSES = R // K_PASS
ROUND_PASSES = 2
ROUNDS = PASSES // ROUND_PASSES
ROUND_R = ROUND_PASSES * K_PASS
MX_BEHIND = 3
PAIR = 2
FIRST_ROUNDS = PAIR
FIRST_PRODUCTS = 3
SCALAR_SORTS = ((3, 0), (3, 1))
SHARED_SORTS = ((2, 1),)
SORTS_FROM = 3
TAIL_PASSES = 2
LAST_HALVES = 2
FINE_ROUNDS = 5
OUT_COLS = 256
M_TILES = N1 * N2 // P
SUMS = ((0, 0, 256), (1, 0, 256), (0, 256, 256), (1, 256, 256))
WEIGHT_ORDER = (0, 2, 1, 3)
M_COLS = N1 * N2
C_TILES = N3 // P
SPLIT = P // N1

FLOPS = 2 * N1 * N2 * N3 * R


def tile_recon_loss_pa_kernel(tc, X, A, B, C, out):
    nc = tc.nc
    with ExitStack() as ctx:
        keep = ctx.enter_context(tc.tile_pool(name="keep", bufs=1))
        prod_pool = ctx.enter_context(tc.tile_pool(name="prod", bufs=3))
        group_pool = ctx.enter_context(tc.tile_pool(name="group", bufs=3))
        res_pool = ctx.enter_context(tc.tile_pool(name="res", bufs=4))
        sort_pool = ctx.enter_context(tc.tile_pool(name="sort", bufs=3))
        last_pool = ctx.enter_context(tc.tile_pool(name="last", bufs=1))
        acc_pool = ctx.enter_context(tc.psum_pool(name="acc", bufs=1))
        turn_pool = ctx.enter_context(tc.psum_pool(name="turn", bufs=4))

        ctx.enter_context(tc.manual_schedule())

        ident = keep.tile([P, P], F32)
        make_identity(nc, ident[:])

        factor_views = [factor.rearrange("i (x w) -> (i x) w", x=SPLIT) for factor in (A, B)]
        factor_raw = {}
        for yh in range(ROUND_PASSES):
            for f in range(2):
                raw = keep.tile([P, K_PASS], BF16, name="factor_raw%d_%d" % (f, yh))
                nc.sync.dma_start(out=raw[:], in_=factor_views[f][:, yh * K_PASS : (yh + 1) * K_PASS])
                factor_raw[(f, yh)] = raw
        c_view = C.rearrange("(a p) r -> p a r", p=P)
        c_raw = []
        for k in range(ROUNDS):
            r_cols = slice(k * ROUND_R, (k + 1) * ROUND_R)
            if k < FINE_ROUNDS:
                pieces = []
                for a in range(C_TILES):
                    c_piece = keep.tile([P, ROUND_R], BF16, name="c_raw%d_%d" % (k, a))
                    nc.sync.dma_start(out=c_piece[:], in_=c_view[:, a, r_cols])
                    pieces.append(c_piece[:])
            else:
                c_chunk = keep.tile([P, C_TILES, ROUND_R], BF16, name="c_raw%d" % k)
                nc.sync.dma_start(out=c_chunk[:], in_=c_view[:, :, r_cols])
                pieces = [c_chunk[:, a, :] for a in range(C_TILES)]
            c_raw.append(pieces)
        x_sb = keep.tile([P, M_TILES, N3], BF16)
        nc.sync.dma_start(out=x_sb[:], in_=X.rearrange("(h i) j k -> (i j) h k", h=M_TILES))

        a_t = keep.tile([P, PASSES * N1 * PACK], BF16)
        b_t = keep.tile([P, PASSES * N2 * PACK], BF16)
        for yh in range(ROUND_PASSES):
            sides = []
            for f, turned in enumerate((a_t, b_t)):
                bank = turn_pool.tile([P, 2, P], F32, tag="bank", name="factor_bank")
                words = factor_raw[(f, yh)][:].bitcast(F32)
                for u in range(2):
                    nc.tensor.transpose(bank[:, u, :], words[:, u : PASS_WORDS : 2], ident[:])
                src = bank[:].rearrange("p u (i x) -> p x i u", x=SPLIT)
                dst = turned[:].bitcast(F32).rearrange("p (yh x i u) -> p yh x i u", x=SPLIT, yh=2, u=2)
                sides.append((src, dst[:, yh]))
            for pieces in (slice(0, FIRST_ROUNDS), slice(FIRST_ROUNDS, SPLIT)):
                for src, dst in sides:
                    nc.scalar.copy(out=dst[:, pieces], in_=src[:, pieces])
        a_by_half = a_t[:].rearrange("p (yh x i t) -> p yh x i t", yh=ROUND_PASSES, i=N1, t=PACK)
        b_by_half = b_t[:].rearrange("p (yh x j t) -> p yh x j t", yh=ROUND_PASSES, j=N2, t=PACK)

        p_pair = {}
        p_codes = {}
        p_scales = {}

        def product(n):
            q, yh = divmod(n, ROUND_PASSES)
            if yh == 0:
                p_pair[q] = prod_pool.tile([P, PAIR * ROUND_PASSES * M_COLS * PACK], BF16, align_bytes=64, name="prod")
            rounds = slice(q * PAIR, (q + 1) * PAIR)
            full = [P, PAIR, N1, N2, PACK]
            by_half = p_pair[q][:].rearrange("p (k yh i j t) -> p yh k i j t", k=PAIR, yh=ROUND_PASSES, i=N1, j=N2)
            nc.vector.tensor_tensor(
                out=by_half[:, yh],
                in0=a_by_half[:, yh, rounds].unsqueeze(3).to_broadcast(full),
                in1=b_by_half[:, yh, rounds].unsqueeze(2).to_broadcast(full),
                op=mybir.AluOpType.mult,
            )

        def quantise_p(k):
            codes = keep.tile([P, ROUND_PASSES * M_COLS], U32, align_bytes=64, name="p_codes%d" % k)
            scales = keep.tile([P, ROUND_PASSES * M_COLS], U8, align_bytes=64, name="p_scales%d" % k)
            q, k_local = divmod(k, PAIR)
            width = ROUND_PASSES * M_COLS * PACK
            nc.vector.quantize_mx(
                out=codes[:].bitcast(FP8X4),
                scales=scales[:],
                in_=p_pair[q][:, k_local * width : (k_local + 1) * width],
            )
            p_codes[k] = codes
            p_scales[k] = scales

        c_grouped = {}
        c_codes = {}
        c_scales = {}

        c_sorted = {}

        def sort_c(k, units, copy):
            a = units[0][0]
            first = units[0][1] * PASS_WORDS
            sorted_words = sort_pool.tile([P, len(units), 2, P], F32, name="sorted%d" % len(units))
            words = c_raw[k][a].bitcast(F32)[:, first : first + len(units) * PASS_WORDS]
            copy(out=sorted_words[:], in_=words.rearrange("p (g w u) -> p g u w", g=len(units), u=2))
            for unit, (a, g_local) in enumerate(units):
                c_sorted[(k, a, g_local)] = sorted_words[:, unit]

        def turn_c(k):
            halves = LAST_HALVES if k == ROUNDS - 1 else 1
            half_tiles = C_TILES // halves
            c_grouped[k] = []
            for half in range(halves):
                if halves == 1:
                    grouped = group_pool.tile([P, ROUND_PASSES * N3 * PACK], BF16, align_bytes=64, name="grouped")
                else:
                    grouped = last_pool.tile(
                        [P, ROUND_PASSES * N3 * PACK // halves], BF16, align_bytes=64, name="last_grouped%d" % half
                    )
                c_grouped[k].append(grouped)
                grouped_words = grouped[:].bitcast(F32).rearrange("p (g n u) -> p g n u", g=ROUND_PASSES, u=2)
                for a_local in range(half_tiles):
                    a = half * half_tiles + a_local
                    bank = turn_pool.tile([P, ROUND_PASSES, 2, P], F32, tag="bank", name="c_bank")
                    words = c_raw[k][a].bitcast(F32)
                    for g_local in range(ROUND_PASSES):
                        first = g_local * PASS_WORDS
                        for u in range(2):
                            if (k, a, g_local) in c_sorted:
                                turned_words = c_sorted[(k, a, g_local)][:, u, :]
                            else:
                                turned_words = words[:, first + u : first + PASS_WORDS : 2]
                            nc.tensor.transpose(bank[:, g_local, u, :], turned_words, ident[:])
                    nc.scalar.copy(
                        out=grouped_words[:, :, a_local * P : (a_local + 1) * P, :],
                        in_=bank[:].rearrange("p g u n -> p g n u"),
                    )

        def new_c_codes(g):
            c_codes[g] = keep.tile([P, N3], U32, align_bytes=64, name="c_codes%d" % g)
            c_scales[g] = keep.tile([P, N3], U8, align_bytes=64, name="c_scales%d" % g)

        def quantise_c(g, half):
            k, g_local = divmod(g, ROUND_PASSES)
            rows = N3 // len(c_grouped[k])
            cols = slice(half * rows, (half + 1) * rows)
            nc.vector.quantize_mx(
                out=c_codes[g][:, cols].bitcast(FP8X4),
                scales=c_scales[g][:, cols],
                in_=c_grouped[k][half][:, g_local * rows * PACK : (g_local + 1) * rows * PACK],
            )

        acc = []
        for number, (h, first, width) in enumerate(SUMS):
            acc.append(acc_pool.tile([P, width], F32, name="acc%d" % number))

        def multiply(g, sums):
            k, g_local = divmod(g, ROUND_PASSES)
            for number in sums:
                h, first, width = SUMS[number]
                cols = slice(g_local * M_COLS + h * P, g_local * M_COLS + (h + 1) * P)
                c_cols = slice(first, first + width)
                nc.tensor.matmul_mx(
                    out=acc[number][:],
                    lhsT=p_codes[k][:, cols].bitcast(FP8X4),
                    lhsT_scale=p_scales[k][:, cols],
                    rhs=c_codes[g][:, c_cols].bitcast(FP8X4),
                    rhs_scale=c_scales[g][:, c_cols],
                    start=(g == 0),
                    stop=(g == PASSES - 1),
                )

        for n in range(FIRST_PRODUCTS):
            product(n)
        quantise_p(0)
        for s in range(ROUNDS + 2):
            if s < ROUNDS:
                turn_c(s)
            if SORTS_FROM <= s + 1 < ROUNDS:
                if (s + 1) % 2 == 1:
                    sort_c(s + 1, SHARED_SORTS, nc.scalar.copy)
                sort_c(s + 1, SCALAR_SORTS, nc.scalar.copy)
            m = s - 1
            if 0 <= m < ROUNDS:
                for g_local in range(ROUND_PASSES):
                    new_c_codes(ROUND_PASSES * m + g_local)
                if 0 < m and m + FIRST_PRODUCTS - 1 < ROUNDS:
                    product(m + FIRST_PRODUCTS - 1)
                if m < ROUNDS - 1:
                    quantise_c(ROUND_PASSES * m, 0)
                    quantise_p(m + 1)
                    quantise_c(ROUND_PASSES * m + 1, 0)
                else:
                    for half in range(LAST_HALVES):
                        for g_local in range(ROUND_PASSES):
                            quantise_c(ROUND_PASSES * m + g_local, half)
                if SORTS_FROM <= m + 2 < ROUNDS and (m + 2) % 2 == 0:
                    sort_c(m + 2, SHARED_SORTS, nc.vector.tensor_copy)
            last_turned = ROUND_PASSES * (s + 1) - 1
            for g in range(last_turned - MX_BEHIND - 1, last_turned - MX_BEHIND + 1):
                if 0 <= g < PASSES - TAIL_PASSES:
                    multiply(g, WEIGHT_ORDER)
        for number in range(len(SUMS)):
            for g in range(PASSES - TAIL_PASSES, PASSES):
                multiply(g, [number])

        out_view = out.rearrange("(h i) j k -> h (i j) k", h=M_TILES)
        for number, (h, start, width) in enumerate(SUMS):
            for first in range(0, width, OUT_COLS):
                cols = slice(start + first, start + first + OUT_COLS)
                res = res_pool.tile([P, OUT_COLS], F32, name="res")
                nc.vector.tensor_tensor(
                    out=res[:],
                    in0=acc[number][:, first : first + OUT_COLS],
                    in1=x_sb[:, h, cols],
                    op=mybir.AluOpType.subtract,
                )
                nc.sync.dma_start(out=out_view[h][:, cols], in_=res[:])
